import numpy as np
import ml_dtypes


def mxq(x, axis, fmt="e4m3"):
    dtype, down = {"e4m3": (ml_dtypes.float8_e4m3fn, 7), "e5m2": (ml_dtypes.float8_e5m2, 14)}[fmt]
    v = np.moveaxis(np.asarray(x, np.float32).astype(ml_dtypes.bfloat16).astype(np.float64), axis, -1)
    blocks = v.reshape(v.shape[:-1] + (-1, 32))
    amax = np.abs(blocks).max(-1, keepdims=True)
    byte = np.maximum(np.where(amax > 0, np.frexp(amax)[1] - 1 + 127, 0) - down, 1)
    scale = np.exp2(byte - 127.0)
    codes = (blocks / scale).astype(np.float32).astype(dtype).astype(np.float64)
    return np.moveaxis((codes * scale).reshape(v.shape), -1, axis)


WIDE = False


def mx_kscale(k):
    if not WIDE:
        return np.ones(k)
    levels = np.array([10, -10, 5, -5, 0])
    a = np.random.permutation(np.resize(levels, k // 512 * 4)).reshape(k // 512, 4)
    idx = np.arange(k)
    return np.exp2(a[idx // 512, idx % 128 // 32])


BF16 = ml_dtypes.bfloat16


def bf(x):
    return np.asarray(x, np.float32).astype(BF16)


def f64(x):
    return np.asarray(x).astype(np.float64)


E2M1 = np.array([0.0, 0.5, 1.0, 1.5, 2.0, 3.0, 4.0, 6.0, -0.0, -0.5, -1.0, -1.5, -2.0, -3.0, -4.0, -6.0])


def pack_weight(w, fmt):
    k, n = w.shape
    w = f64(bf(w)).reshape(k // 32, 32, n)
    amax = np.abs(w).max(1)
    if fmt == "e4m3":
        byte = np.frexp(amax)[1] - 1 + 127 - 7
    else:
        mant, ex = np.frexp(amax / 6.0)
        byte = np.where(mant > 0.5, ex, ex - 1) + 127
    byte = np.clip(np.where(amax > 0, byte, 1), 1, 254)
    scaled = (w * np.exp2(127.0 - byte)[:, None, :]).reshape(k, n).astype(np.float32)
    by_word = np.ascontiguousarray(scaled.reshape(k // 512, 128, 4, n).transpose(0, 1, 3, 2))
    if fmt == "e4m3":
        words = by_word.astype(ml_dtypes.float8_e4m3fn).view(np.uint8)
    else:
        c = by_word.astype(ml_dtypes.float4_e2m1fn).view(np.uint8) & 0xF
        words = c[..., 0::2] | (c[..., 1::2] << 4)
    return np.ascontiguousarray(words), np.ascontiguousarray(byte.astype(np.uint8).reshape(k // 512, 16, n))


def unpack_weight(words, scales, fmt):
    g, p, n, _ = words.shape
    if fmt == "e4m3":
        vals = np.ascontiguousarray(words).view(ml_dtypes.float8_e4m3fn).astype(np.float64)
    else:
        nib = np.empty((g, p, n, 4), np.uint8)
        nib[..., 0::2] = words & 0xF
        nib[..., 1::2] = words >> 4
        vals = E2M1[nib]
    vals = vals * np.repeat(np.exp2(scales.astype(np.float64) - 127.0), 8, axis=1)[..., None]
    return vals.transpose(0, 1, 3, 2).reshape(g * 512, n)


B, S, M, D, H = 1, 128, 2, 8192, 1536
FMT = "e4m3"


def setup_inputs():
    s = mx_kscale(2 * D)
    lens = np.random.randint(0, M + 1, (B, S))
    valid = (np.arange(M)[None, None, :] < lens[:, :, None]).astype(np.float64)
    src = np.random.standard_normal((B, S, M, D)) / np.sqrt(M) * s[:D]
    neigh = np.random.standard_normal((B, S, M, D)) * 2.0 * valid[..., None] * s[D:]
    words, scales = pack_weight(np.random.standard_normal((2 * D, H)) / np.sqrt(2 * D) / s[:, None], FMT)
    return {"src_node_features": bf(src), "neigh_node_features": bf(neigh),
            "W_map_words": words, "W_map_scales": scales,
            "b_map": bf(-0.5 + 0.3 * np.random.standard_normal(H))}


def reference(src_node_features, neigh_node_features, W_map_words, W_map_scales, b_map):
    src, neigh = f64(src_node_features), f64(neigh_node_features)
    valid = np.any(neigh != 0, axis=-1)
    num = np.sum(valid, axis=-1).astype(np.float64)
    neigh_mean = neigh.sum(axis=2) / np.maximum(num, 1.0)[..., None]
    hidden = np.concatenate([src.sum(axis=2), neigh_mean], axis=-1)
    hidden = hidden.reshape(-1, hidden.shape[-1])
    v = (mxq(hidden, 1, "e4m3") @ unpack_weight(W_map_words, W_map_scales, FMT)) + f64(b_map)
    return np.where(v >= 0, v, 0.01 * v)

@@ -1,0 +1,228 @@
+from contextlib import ExitStack
+
+import concourse.mybir as mybir
+from concourse.masks import make_identity
+
+BF16 = mybir.dt.bfloat16
+F32 = mybir.dt.float32
+I32 = mybir.dt.int32
+U32 = mybir.dt.uint32
+U8 = mybir.dt.uint8
+FP8X4 = mybir.dt.float8_e4m3fn_x4
+ALU = mybir.AluOpType
+ACT = mybir.ActivationFunctionType
+AXIS = mybir.AxisListType
+
+P = 128
+SLOTS = 2
+D = 8192
+H = 1536
+PACK = 4
+K_PASS = P * PACK
+PASSES = 2 * D // K_PASS
+SRC_PASSES = D // K_PASS
+N_TILE = 512
+N_BLOCKS = H // N_TILE
+CHUNK = 2048
+CHUNK_PASSES = CHUNK // K_PASS
+CHUNKS = D // CHUNK
+BANK_PASSES = 2
+PLANES_PER_TILE = 4
+PLANE_SETS = PASSES // PLANES_PER_TILE
+QUADRANT = 32
+LIVE_ROWS = 4
+W_BUFS = 10
+TAPER_PASSES = 2
+SLOPE = 0.01
+
+FLOPS = 2 * P * 2 * D * H
+
+
+def tile_syntacticgcn_k_kernel(
+    tc, src_node_features, neigh_node_features, W_map_words, W_map_scales, b_map, out
+):
+    nc = tc.nc
+    with ExitStack() as ctx:
+        ctx.enter_context(tc.manual_schedule())
+        keep = ctx.enter_context(tc.tile_pool(name="keep", bufs=1))
+        work = ctx.enter_context(tc.tile_pool(name="work", bufs=2))
+        w_pool = ctx.enter_context(tc.tile_pool(name="weights", bufs=W_BUFS))
+        tail_pool = ctx.enter_context(tc.tile_pool(name="tail_weights", bufs=N_BLOCKS))
+        acc_pool = ctx.enter_context(tc.psum_pool(name="acc", bufs=1))
+        xt_pool = ctx.enter_context(tc.psum_pool(name="xt", bufs=4))
+
+        def load_slots(features, label):
+            by_slot = features.rearrange("b n s d -> s (b n) d")
+            slot_tiles = []
+            for s in range(SLOTS):
+                slot_tile = keep.tile([P, D], BF16, name="%s_slot%d" % (label, s))
+                nc.sync.dma_start(out=slot_tile[:], in_=by_slot[s])
+                slot_tiles.append(slot_tile)
+            return slot_tiles
+
+        src_slot = load_slots(src_node_features, "src")
+
+        bias_row = keep.tile([P, H], BF16)
+        nc.vector.memset(bias_row[:], 0.0)
+        nc.sync.dma_start(out=bias_row[0:1, :], in_=b_map.rearrange("(o h) -> o h", o=1))
+        ones = keep.tile([P, P], BF16)
+        nc.vector.memset(ones[:], 1.0)
+        ident = keep.tile([P, P], BF16)
+        make_identity(nc, ident[:])
+
+        neigh_slot = load_slots(neigh_node_features, "neigh")
+
+        w_planes = keep.tile([P, PLANE_SETS, H], U8, align_bytes=64)
+        nc.vector.memset(w_planes[:].rearrange("p s h -> p (s h)").bitcast(I32), 0)
+        scale_rows = W_map_scales.bitcast(I32)
+        for s in range(PLANE_SETS):
+            for quad in range(P // QUADRANT):
+                nc.sync.dma_start(
+                    out=w_planes[
+                        quad * QUADRANT : quad * QUADRANT + PLANES_PER_TILE * LIVE_ROWS, s, :
+                    ].bitcast(I32),
+                    in_=scale_rows[
+                        s * PLANES_PER_TILE : (s + 1) * PLANES_PER_TILE,
+                        quad * LIVE_ROWS : (quad + 1) * LIVE_ROWS,
+                        :,
+                    ],
+                )
+
+        abs_sums = keep.tile([P, SLOTS, CHUNKS], F32)
+        for s in range(SLOTS):
+            for c in range(CHUNKS):
+                unread = work.tile([P, CHUNK], BF16)
+                nc.scalar.activation(
+                    out=unread[:],
+                    in_=neigh_slot[s][:, c * CHUNK : (c + 1) * CHUNK],
+                    func=ACT.Abs,
+                    accum_out=abs_sums[:, s, c : c + 1],
+                )
+
+        codes = keep.tile([P, PASSES * P], U32, align_bytes=64)
+        code_scales = keep.tile([P, PASSES * P], U8, align_bytes=64)
+
+        def quantise_chunk(hidden_chunk, first_pass):
+            grouped = work.tile([P, CHUNK_PASSES, P, PACK], BF16, align_bytes=64)
+            for bank in range(CHUNK_PASSES // BANK_PASSES):
+                xt = xt_pool.tile([P, BANK_PASSES, PACK, P], BF16, tag="xt")
+                for i in range(BANK_PASSES):
+                    first_col = (bank * BANK_PASSES + i) * K_PASS
+                    for t in range(PACK):
+                        nc.tensor.transpose(
+                            xt[:, i, t, :],
+                            hidden_chunk[:, first_col + t : first_col + K_PASS : PACK],
+                            ident[:],
+                        )
+                nc.vector.tensor_copy(
+                    out=grouped[:, bank * BANK_PASSES : (bank + 1) * BANK_PASSES, :, :],
+                    in_=xt[:].rearrange("p i t r -> p i r t"),
+                )
+            cols = slice(first_pass * P, (first_pass + CHUNK_PASSES) * P)
+            nc.vector.quantize_mx(
+                out=codes[:, cols].bitcast(FP8X4),
+                scales=code_scales[:, cols],
+                in_=grouped[:].rearrange("p g r t -> p (g r t)"),
+            )
+
+        def sum_of_src(c):
+            cols = slice(c * CHUNK, (c + 1) * CHUNK)
+            a_chunk = work.tile([P, CHUNK], BF16, tag="hidden_chunk")
+            nc.vector.tensor_tensor(
+                out=a_chunk[:], in0=src_slot[0][:, cols], in1=src_slot[1][:, cols], op=ALU.add
+            )
+            return a_chunk
+
+        a_chunks = [sum_of_src(0)]
+        for c in range(CHUNKS):
+            if c + 1 < CHUNKS:
+                a_chunks.append(sum_of_src(c + 1))
+            quantise_chunk(a_chunks[c], c * CHUNK_PASSES)
+
+        bias_all = keep.tile([P, H], F32)
+        for n in range(N_BLOCKS):
+            cols = slice(n * N_TILE, (n + 1) * N_TILE)
+            bias_ps = xt_pool.tile([P, N_TILE], F32, tag="xt")
+            nc.tensor.matmul(
+                out=bias_ps[:], lhsT=ones[:], rhs=bias_row[:, cols], start=True, stop=True
+            )
+            nc.vector.tensor_copy(out=bias_all[:, cols], in_=bias_ps[:])
+
+        slot_sums = keep.tile([P, SLOTS], F32)
+        nc.vector.tensor_reduce(out=slot_sums[:], in_=abs_sums[:], axis=AXIS.X, op=ALU.add)
+        slot_counts = keep.tile([P, SLOTS], F32)
+        nc.vector.tensor_single_scalar(out=slot_counts[:], in_=slot_sums[:], scalar=0.0, op=ALU.is_gt)
+        num = keep.tile([P, 1], F32)
+        nc.vector.tensor_reduce(out=num[:], in_=slot_counts[:], axis=AXIS.X, op=ALU.add)
+        divisor = keep.tile([P, 1], F32)
+        nc.vector.tensor_scalar_max(out=divisor[:], in0=num[:], scalar1=1.0)
+        one_over_num = keep.tile([P, 1], F32)
+        nc.vector.reciprocal(out=one_over_num[:], in_=divisor[:])
+
+        def mean_of_neigh(c):
+            cols = slice(c * CHUNK, (c + 1) * CHUNK)
+            slot_sum = work.tile([P, CHUNK], F32)
+            nc.vector.tensor_tensor(
+                out=slot_sum[:], in0=neigh_slot[0][:, cols], in1=neigh_slot[1][:, cols], op=ALU.add
+            )
+            m_chunk = work.tile([P, CHUNK], BF16, tag="hidden_chunk")
+            nc.scalar.activation(
+                out=m_chunk[:], in_=slot_sum[:], func=ACT.Copy, scale=one_over_num[:, 0:1]
+            )
+            return m_chunk
+
+        acc = [acc_pool.tile([P, N_TILE], F32, name="acc%d" % n) for n in range(N_BLOCKS)]
+
+        def mx_pass(g, n, w_words):
+            s, i = divmod(g, PLANES_PER_TILE)
+            nc.tensor.matmul_mx(
+                out=acc[n][:],
+                lhsT=codes[:, g * P : (g + 1) * P].bitcast(FP8X4),
+                lhsT_scale=code_scales[:, g * P : (g + 1) * P],
+                rhs=w_words.bitcast(FP8X4),
+                rhs_scale=w_planes[i * LIVE_ROWS : P, s, n * N_TILE : (n + 1) * N_TILE],
+                start=(g == 0),
+                stop=(g == PASSES - 1),
+            )
+
+        def whole_pass(g):
+            w_words = w_pool.tile([P, H], U32, align_bytes=64)
+            nc.sync.dma_start(
+                out=w_words[:].bitcast(I32),
+                in_=W_map_words[g].rearrange("p h t -> p (h t)").bitcast(I32),
+            )
+            for n in range(N_BLOCKS):
+                mx_pass(g, n, w_words[:, n * N_TILE : (n + 1) * N_TILE])
+
+        m_chunks = [mean_of_neigh(0)]
+        for c in range(CHUNKS):
+            for g in range(c * CHUNK_PASSES, (c + 1) * CHUNK_PASSES):
+                whole_pass(g)
+            if c + 1 < CHUNKS:
+                m_chunks.append(mean_of_neigh(c + 1))
+            quantise_chunk(m_chunks[c], SRC_PASSES + c * CHUNK_PASSES)
+        for g in range(SRC_PASSES, PASSES - TAPER_PASSES):
+            whole_pass(g)
+
+        first_tail = PASSES - TAPER_PASSES
+        tail_words = []
+        for n in range(N_BLOCKS):
+            w_tail = tail_pool.tile([P, TAPER_PASSES, N_TILE], U32, align_bytes=64)
+            nc.sync.dma_start(
+                out=w_tail[:].bitcast(I32),
+                in_=W_map_words[first_tail:PASSES, :, n * N_TILE : (n + 1) * N_TILE, :]
+                .rearrange("g p h t -> p g (h t)")
+                .bitcast(I32),
+            )
+            tail_words.append(w_tail)
+        for n in range(N_BLOCKS):
+            cols = slice(n * N_TILE, (n + 1) * N_TILE)
+            for i in range(TAPER_PASSES):
+                mx_pass(first_tail + i, n, tail_words[n][:, i, :])
+            biased = work.tile([P, N_TILE], F32)
+            nc.vector.tensor_tensor(out=biased[:], in0=acc[n][:], in1=bias_all[:, cols], op=ALU.add)
+            result = work.tile([P, N_TILE], F32)
+            nc.vector.scalar_tensor_tensor(
+                out=result[:], in0=biased[:], scalar=SLOPE, in1=biased[:], op0=ALU.mult, op1=ALU.max
+            )
+            nc.sync.dma_start(out=out[:, cols], in_=result[:])

@@ -74,18 +74,17 @@ def tile_syntacticgcn_k_kernel(
 
         w_planes = keep.tile([P, PLANE_SETS, H], U8, align_bytes=64)
         nc.vector.memset(w_planes[:].rearrange("p s h -> p (s h)").bitcast(I32), 0)
-        scale_rows = W_map_scales.bitcast(I32)
-        for s in range(PLANE_SETS):
-            for quad in range(P // QUADRANT):
+        scale_rows = W_map_scales.bitcast(I32).rearrange(
+            "(s i) q n -> q i s n", i=PLANES_PER_TILE
+        )
+        for quad in range(P // QUADRANT):
+            for j in range(LIVE_ROWS):
+                first = quad * QUADRANT + j
                 nc.sync.dma_start(
                     out=w_planes[
-                        quad * QUADRANT : quad * QUADRANT + PLANES_PER_TILE * LIVE_ROWS, s, :
+                        first : quad * QUADRANT + PLANES_PER_TILE * LIVE_ROWS : LIVE_ROWS, :, :
                     ].bitcast(I32),
-                    in_=scale_rows[
-                        s * PLANES_PER_TILE : (s + 1) * PLANES_PER_TILE,
-                        quad * LIVE_ROWS : (quad + 1) * LIVE_ROWS,
-                        :,
-                    ],
+                    in_=scale_rows[quad * LIVE_ROWS + j],
                 )
 
         abs_sums = keep.tile([P, SLOTS, CHUNKS], F32)

@@ -77,7 +77,7 @@ def tile_syntacticgcn_k_kernel(
         scale_rows = W_map_scales.bitcast(I32).rearrange(
             "(s i) q n -> q i s n", i=PLANES_PER_TILE
         )
-        for quad in range(P // QUADRANT):
+        for quad in (2, 3, 0, 1):
             for j in range(LIVE_ROWS):
                 first = quad * QUADRANT + j
                 nc.sync.dma_start(

@@ -31,7 +31,8 @@ PLANES_PER_TILE = 4
 PLANE_SETS = PASSES // PLANES_PER_TILE
 QUADRANT = 32
 LIVE_ROWS = 4
-W_BUFS = 10
+W_LOAD_PASSES = 2
+W_BUFS = 5
 TAPER_PASSES = 2
 SLOPE = 0.01
 
@@ -184,24 +185,27 @@ def tile_syntacticgcn_k_kernel(
                 stop=(g == PASSES - 1),
             )
 
-        def whole_pass(g):
-            w_words = w_pool.tile([P, H], U32, align_bytes=64)
+        def whole_passes(first_pass):
+            w_words = w_pool.tile([P, W_LOAD_PASSES, H], U32, align_bytes=64)
             nc.sync.dma_start(
                 out=w_words[:].bitcast(I32),
-                in_=W_map_words[g].rearrange("p h t -> p (h t)").bitcast(I32),
+                in_=W_map_words[first_pass : first_pass + W_LOAD_PASSES]
+                .rearrange("g p h t -> p g (h t)")
+                .bitcast(I32),
             )
-            for n in range(N_BLOCKS):
-                mx_pass(g, n, w_words[:, n * N_TILE : (n + 1) * N_TILE])
+            for i in range(W_LOAD_PASSES):
+                for n in range(N_BLOCKS):
+                    mx_pass(first_pass + i, n, w_words[:, i, n * N_TILE : (n + 1) * N_TILE])
 
         m_chunks = [mean_of_neigh(0)]
         for c in range(CHUNKS):
-            for g in range(c * CHUNK_PASSES, (c + 1) * CHUNK_PASSES):
-                whole_pass(g)
+            for g in range(c * CHUNK_PASSES, (c + 1) * CHUNK_PASSES, W_LOAD_PASSES):
+                whole_passes(g)
             if c + 1 < CHUNKS:
                 m_chunks.append(mean_of_neigh(c + 1))
             quantise_chunk(m_chunks[c], SRC_PASSES + c * CHUNK_PASSES)
-        for g in range(SRC_PASSES, PASSES - TAPER_PASSES):
-            whole_pass(g)
+        for g in range(SRC_PASSES, PASSES - TAPER_PASSES, W_LOAD_PASSES):
+            whole_passes(g)
 
         first_tail = PASSES - TAPER_PASSES
         tail_words = []

@@ -31,8 +31,9 @@ PLANES_PER_TILE = 4
 PLANE_SETS = PASSES // PLANES_PER_TILE
 QUADRANT = 32
 LIVE_ROWS = 4
-W_LOAD_PASSES = 2
-W_BUFS = 5
+W_LOAD_PASSES = 4
+SHRINKING_LOADS = (2, 2, 1, 1)
+W_BUFS = 3
 TAPER_PASSES = 2
 SLOPE = 0.01
 
@@ -91,7 +92,7 @@ def tile_syntacticgcn_k_kernel(
         abs_sums = keep.tile([P, SLOTS, CHUNKS], F32)
         for s in range(SLOTS):
             for c in range(CHUNKS):
-                unread = work.tile([P, CHUNK], BF16)
+                unread = keep.tile([P, CHUNK], BF16, name="unread")
                 nc.scalar.activation(
                     out=unread[:],
                     in_=neigh_slot[s][:, c * CHUNK : (c + 1) * CHUNK],
@@ -185,29 +186,31 @@ def tile_syntacticgcn_k_kernel(
                 stop=(g == PASSES - 1),
             )
 
-        def whole_passes(first_pass):
+        def whole_passes(first_pass, count):
             w_words = w_pool.tile([P, W_LOAD_PASSES, H], U32, align_bytes=64)
             nc.sync.dma_start(
-                out=w_words[:].bitcast(I32),
-                in_=W_map_words[first_pass : first_pass + W_LOAD_PASSES]
+                out=w_words[:, 0:count, :].bitcast(I32),
+                in_=W_map_words[first_pass : first_pass + count]
                 .rearrange("g p h t -> p g (h t)")
                 .bitcast(I32),
             )
-            for i in range(W_LOAD_PASSES):
+            for i in range(count):
                 for n in range(N_BLOCKS):
                     mx_pass(first_pass + i, n, w_words[:, i, n * N_TILE : (n + 1) * N_TILE])
 
         m_chunks = [mean_of_neigh(0)]
         for c in range(CHUNKS):
-            for g in range(c * CHUNK_PASSES, (c + 1) * CHUNK_PASSES, W_LOAD_PASSES):
-                whole_passes(g)
+            whole_passes(c * W_LOAD_PASSES, W_LOAD_PASSES)
             if c + 1 < CHUNKS:
                 m_chunks.append(mean_of_neigh(c + 1))
             quantise_chunk(m_chunks[c], SRC_PASSES + c * CHUNK_PASSES)
-        for g in range(SRC_PASSES, PASSES - TAPER_PASSES, W_LOAD_PASSES):
-            whole_passes(g)
-
         first_tail = PASSES - TAPER_PASSES
+        first_shrinking = first_tail - sum(SHRINKING_LOADS)
+        for g in range(SRC_PASSES, first_shrinking, W_LOAD_PASSES):
+            whole_passes(g, W_LOAD_PASSES)
+        for i, count in enumerate(SHRINKING_LOADS):
+            whole_passes(first_shrinking + sum(SHRINKING_LOADS[:i]), count)
+
         tail_words = []
         for n in range(N_BLOCKS):
             w_tail = tail_pool.tile([P, TAPER_PASSES, N_TILE], U32, align_bytes=64)

@@ -32,9 +32,10 @@ PLANE_SETS = PASSES // PLANES_PER_TILE
 QUADRANT = 32
 LIVE_ROWS = 4
 W_LOAD_PASSES = 4
-SHRINKING_LOADS = (2, 2, 1, 1)
+SHRINKING_LOADS = (2, 2, 1)
 W_BUFS = 3
-TAPER_PASSES = 2
+TAPER_PASSES = 3
+LAST_PARTS = 2
 SLOPE = 0.01
 
 FLOPS = 2 * P * 2 * D * H
@@ -92,7 +93,7 @@ def tile_syntacticgcn_k_kernel(
         abs_sums = keep.tile([P, SLOTS, CHUNKS], F32)
         for s in range(SLOTS):
             for c in range(CHUNKS):
-                unread = keep.tile([P, CHUNK], BF16, name="unread")
+                unread = work.tile([P, CHUNK], BF16, tag="slot_sum")
                 nc.scalar.activation(
                     out=unread[:],
                     in_=neigh_slot[s][:, c * CHUNK : (c + 1) * CHUNK],
@@ -162,7 +163,7 @@ def tile_syntacticgcn_k_kernel(
 
         def mean_of_neigh(c):
             cols = slice(c * CHUNK, (c + 1) * CHUNK)
-            slot_sum = work.tile([P, CHUNK], F32)
+            slot_sum = work.tile([P, CHUNK], F32, tag="slot_sum")
             nc.vector.tensor_tensor(
                 out=slot_sum[:], in0=neigh_slot[0][:, cols], in1=neigh_slot[1][:, cols], op=ALU.add
             )
@@ -222,13 +223,28 @@ def tile_syntacticgcn_k_kernel(
             )
             tail_words.append(w_tail)
         for n in range(N_BLOCKS):
-            cols = slice(n * N_TILE, (n + 1) * N_TILE)
             for i in range(TAPER_PASSES):
                 mx_pass(first_tail + i, n, tail_words[n][:, i, :])
+            part = N_TILE // (LAST_PARTS if n == N_BLOCKS - 1 else 1)
+            first_cols = range(n * N_TILE, (n + 1) * N_TILE, part)
             biased = work.tile([P, N_TILE], F32)
-            nc.vector.tensor_tensor(out=biased[:], in0=acc[n][:], in1=bias_all[:, cols], op=ALU.add)
             result = work.tile([P, N_TILE], F32)
-            nc.vector.scalar_tensor_tensor(
-                out=result[:], in0=biased[:], scalar=SLOPE, in1=biased[:], op0=ALU.mult, op1=ALU.max
-            )
-            nc.sync.dma_start(out=out[:, cols], in_=result[:])
+            for first in first_cols:
+                local = slice(first - n * N_TILE, first - n * N_TILE + part)
+                nc.vector.tensor_tensor(
+                    out=biased[:, local],
+                    in0=acc[n][:, local],
+                    in1=bias_all[:, first : first + part],
+                    op=ALU.add,
+                )
+            for first in first_cols:
+                local = slice(first - n * N_TILE, first - n * N_TILE + part)
+                nc.vector.scalar_tensor_tensor(
+                    out=result[:, local],
+                    in0=biased[:, local],
+                    scalar=SLOPE,
+                    in1=biased[:, local],
+                    op0=ALU.mult,
+                    op1=ALU.max,
+                )
+                nc.sync.dma_start(out=out[:, first : first + part], in_=result[:, local])

@@ -23,6 +23,11 @@ PASSES = 2 * D // K_PASS
 SRC_PASSES = D // K_PASS
 N_TILE = 512
 N_BLOCKS = H // N_TILE
+OUT_WIDTHS = (512, 512, 256, 256)
+OUT_COLS = tuple(
+    slice(sum(OUT_WIDTHS[:n]), sum(OUT_WIDTHS[: n + 1])) for n in range(len(OUT_WIDTHS))
+)
+BLOCK_PARTS = ((0,), (1,), (2, 3))
 CHUNK = 2048
 CHUNK_PASSES = CHUNK // K_PASS
 CHUNKS = D // CHUNK
@@ -35,7 +40,6 @@ W_LOAD_PASSES = 4
 SHRINKING_LOADS = (2, 2, 1)
 W_BUFS = 3
 TAPER_PASSES = 3
-LAST_PARTS = 2
 SLOPE = 0.01
 
 FLOPS = 2 * P * 2 * D * H
@@ -173,7 +177,9 @@ def tile_syntacticgcn_k_kernel(
             )
             return m_chunk
 
-        acc = [acc_pool.tile([P, N_TILE], F32, name="acc%d" % n) for n in range(N_BLOCKS)]
+        acc = [
+            acc_pool.tile([P, width], F32, name="acc%d" % n) for n, width in enumerate(OUT_WIDTHS)
+        ]
 
         def mx_pass(g, n, w_words):
             s, i = divmod(g, PLANES_PER_TILE)
@@ -182,7 +188,7 @@ def tile_syntacticgcn_k_kernel(
                 lhsT=codes[:, g * P : (g + 1) * P].bitcast(FP8X4),
                 lhsT_scale=code_scales[:, g * P : (g + 1) * P],
                 rhs=w_words.bitcast(FP8X4),
-                rhs_scale=w_planes[i * LIVE_ROWS : P, s, n * N_TILE : (n + 1) * N_TILE],
+                rhs_scale=w_planes[i * LIVE_ROWS : P, s, OUT_COLS[n]],
                 start=(g == 0),
                 stop=(g == PASSES - 1),
             )
@@ -196,8 +202,8 @@ def tile_syntacticgcn_k_kernel(
                 .bitcast(I32),
             )
             for i in range(count):
-                for n in range(N_BLOCKS):
-                    mx_pass(first_pass + i, n, w_words[:, i, n * N_TILE : (n + 1) * N_TILE])
+                for n, cols in enumerate(OUT_COLS):
+                    mx_pass(first_pass + i, n, w_words[:, i, cols])
 
         m_chunks = [mean_of_neigh(0)]
         for c in range(CHUNKS):
@@ -222,29 +228,31 @@ def tile_syntacticgcn_k_kernel(
                 .bitcast(I32),
             )
             tail_words.append(w_tail)
-        for n in range(N_BLOCKS):
-            for i in range(TAPER_PASSES):
-                mx_pass(first_tail + i, n, tail_words[n][:, i, :])
-            part = N_TILE // (LAST_PARTS if n == N_BLOCKS - 1 else 1)
-            first_cols = range(n * N_TILE, (n + 1) * N_TILE, part)
+        for block, parts in enumerate(BLOCK_PARTS):
             biased = work.tile([P, N_TILE], F32)
             result = work.tile([P, N_TILE], F32)
-            for first in first_cols:
-                local = slice(first - n * N_TILE, first - n * N_TILE + part)
+
+            def in_block(n):
+                first = OUT_COLS[n].start - block * N_TILE
+                return slice(first, first + OUT_WIDTHS[n])
+
+            for n in parts:
+                for i in range(TAPER_PASSES):
+                    mx_pass(first_tail + i, n, tail_words[block][:, i, in_block(n)])
+            for n in parts:
                 nc.vector.tensor_tensor(
-                    out=biased[:, local],
-                    in0=acc[n][:, local],
-                    in1=bias_all[:, first : first + part],
+                    out=biased[:, in_block(n)],
+                    in0=acc[n][:],
+                    in1=bias_all[:, OUT_COLS[n]],
                     op=ALU.add,
                 )
-            for first in first_cols:
-                local = slice(first - n * N_TILE, first - n * N_TILE + part)
+            for n in parts:
                 nc.vector.scalar_tensor_tensor(
-                    out=result[:, local],
-                    in0=biased[:, local],
+                    out=result[:, in_block(n)],
+                    in0=biased[:, in_block(n)],
                     scalar=SLOPE,
-                    in1=biased[:, local],
+                    in1=biased[:, in_block(n)],
                     op0=ALU.mult,
                     op1=ALU.max,
                 )
-                nc.sync.dma_start(out=out[:, first : first + part], in_=result[:, local])
+                nc.sync.dma_start(out=out[:, OUT_COLS[n]], in_=result[:, in_block(n)])

from contextlib import ExitStack

import concourse.mybir as mybir
from concourse.masks import make_identity

BF16 = mybir.dt.bfloat16
F32 = mybir.dt.float32
I32 = mybir.dt.int32
U32 = mybir.dt.uint32
U8 = mybir.dt.uint8
FP8X4 = mybir.dt.float8_e4m3fn_x4
ALU = mybir.AluOpType
ACT = mybir.ActivationFunctionType
AXIS = mybir.AxisListType

P = 128
SLOTS = 2
D = 8192
H = 1536
PACK = 4
K_PASS = P * PACK
PASSES = 2 * D // K_PASS
SRC_PASSES = D // K_PASS
N_TILE = 512
N_BLOCKS = H // N_TILE
OUT_WIDTHS = (512, 512, 256, 256)
OUT_COLS = tuple(
    slice(sum(OUT_WIDTHS[:n]), sum(OUT_WIDTHS[: n + 1])) for n in range(len(OUT_WIDTHS))
)
BLOCK_PARTS = ((0,), (1,), (2, 3))
CHUNK = 2048
CHUNK_PASSES = CHUNK // K_PASS
CHUNKS = D // CHUNK
BANK_PASSES = 2
PLANES_PER_TILE = 4
PLANE_SETS = PASSES // PLANES_PER_TILE
QUADRANT = 32
LIVE_ROWS = 4
W_LOAD_PASSES = 4
SHRINKING_LOADS = (2, 2, 1)
W_BUFS = 3
TAPER_PASSES = 3
SLOPE = 0.01

FLOPS = 2 * P * 2 * D * H


def tile_syntacticgcn_k_kernel(
    tc, src_node_features, neigh_node_features, W_map_words, W_map_scales, b_map, out
):
    nc = tc.nc
    with ExitStack() as ctx:
        ctx.enter_context(tc.manual_schedule())
        keep = ctx.enter_context(tc.tile_pool(name="keep", bufs=1))
        work = ctx.enter_context(tc.tile_pool(name="work", bufs=2))
        w_pool = ctx.enter_context(tc.tile_pool(name="weights", bufs=W_BUFS))
        tail_pool = ctx.enter_context(tc.tile_pool(name="tail_weights", bufs=N_BLOCKS))
        acc_pool = ctx.enter_context(tc.psum_pool(name="acc", bufs=1))
        xt_pool = ctx.enter_context(tc.psum_pool(name="xt", bufs=4))

        def load_slots(features, label):
            by_slot = features.rearrange("b n s d -> s (b n) d")
            slot_tiles = []
            for s in range(SLOTS):
                slot_tile = keep.tile([P, D], BF16, name="%s_slot%d" % (label, s))
                nc.sync.dma_start(out=slot_tile[:], in_=by_slot[s])
                slot_tiles.append(slot_tile)
            return slot_tiles

        src_slot = load_slots(src_node_features, "src")

        bias_row = keep.tile([P, H], BF16)
        nc.vector.memset(bias_row[:], 0.0)
        nc.sync.dma_start(out=bias_row[0:1, :], in_=b_map.rearrange("(o h) -> o h", o=1))
        ones = keep.tile([P, P], BF16)
        nc.vector.memset(ones[:], 1.0)
        ident = keep.tile([P, P], BF16)
        make_identity(nc, ident[:])

        neigh_slot = load_slots(neigh_node_features, "neigh")

        w_planes = keep.tile([P, PLANE_SETS, H], U8, align_bytes=64)
        nc.vector.memset(w_planes[:].rearrange("p s h -> p (s h)").bitcast(I32), 0)
        scale_rows = W_map_scales.bitcast(I32).rearrange(
            "(s i) q n -> q i s n", i=PLANES_PER_TILE
        )
        for quad in (2, 3, 0, 1):
            for j in range(LIVE_ROWS):
                first = quad * QUADRANT + j
                nc.sync.dma_start(
                    out=w_planes[
                        first : quad * QUADRANT + PLANES_PER_TILE * LIVE_ROWS : LIVE_ROWS, :, :
                    ].bitcast(I32),
                    in_=scale_rows[quad * LIVE_ROWS + j],
                )

        abs_sums = keep.tile([P, SLOTS, CHUNKS], F32)
        for s in range(SLOTS):
            for c in range(CHUNKS):
                unread = work.tile([P, CHUNK], BF16, tag="slot_sum")
                nc.scalar.activation(
                    out=unread[:],
                    in_=neigh_slot[s][:, c * CHUNK : (c + 1) * CHUNK],
                    func=ACT.Abs,
                    accum_out=abs_sums[:, s, c : c + 1],
                )

        codes = keep.tile([P, PASSES * P], U32, align_bytes=64)
        code_scales = keep.tile([P, PASSES * P], U8, align_bytes=64)

        def quantise_chunk(hidden_chunk, first_pass):
            grouped = work.tile([P, CHUNK_PASSES, P, PACK], BF16, align_bytes=64)
            for bank in range(CHUNK_PASSES // BANK_PASSES):
                xt = xt_pool.tile([P, BANK_PASSES, PACK, P], BF16, tag="xt")
                for i in range(BANK_PASSES):
                    first_col = (bank * BANK_PASSES + i) * K_PASS
                    for t in range(PACK):
                        nc.tensor.transpose(
                            xt[:, i, t, :],
                            hidden_chunk[:, first_col + t : first_col + K_PASS : PACK],
                            ident[:],
                        )
                nc.vector.tensor_copy(
                    out=grouped[:, bank * BANK_PASSES : (bank + 1) * BANK_PASSES, :, :],
                    in_=xt[:].rearrange("p i t r -> p i r t"),
                )
            cols = slice(first_pass * P, (first_pass + CHUNK_PASSES) * P)
            nc.vector.quantize_mx(
                out=codes[:, cols].bitcast(FP8X4),
                scales=code_scales[:, cols],
                in_=grouped[:].rearrange("p g r t -> p (g r t)"),
            )

        def sum_of_src(c):
            cols = slice(c * CHUNK, (c + 1) * CHUNK)
            a_chunk = work.tile([P, CHUNK], BF16, tag="hidden_chunk")
            nc.vector.tensor_tensor(
                out=a_chunk[:], in0=src_slot[0][:, cols], in1=src_slot[1][:, cols], op=ALU.add
            )
            return a_chunk

        a_chunks = [sum_of_src(0)]
        for c in range(CHUNKS):
            if c + 1 < CHUNKS:
                a_chunks.append(sum_of_src(c + 1))
            quantise_chunk(a_chunks[c], c * CHUNK_PASSES)

        bias_all = keep.tile([P, H], F32)
        for n in range(N_BLOCKS):
            cols = slice(n * N_TILE, (n + 1) * N_TILE)
            bias_ps = xt_pool.tile([P, N_TILE], F32, tag="xt")
            nc.tensor.matmul(
                out=bias_ps[:], lhsT=ones[:], rhs=bias_row[:, cols], start=True, stop=True
            )
            nc.vector.tensor_copy(out=bias_all[:, cols], in_=bias_ps[:])

        slot_sums = keep.tile([P, SLOTS], F32)
        nc.vector.tensor_reduce(out=slot_sums[:], in_=abs_sums[:], axis=AXIS.X, op=ALU.add)
        slot_counts = keep.tile([P, SLOTS], F32)
        nc.vector.tensor_single_scalar(out=slot_counts[:], in_=slot_sums[:], scalar=0.0, op=ALU.is_gt)
        num = keep.tile([P, 1], F32)
        nc.vector.tensor_reduce(out=num[:], in_=slot_counts[:], axis=AXIS.X, op=ALU.add)
        divisor = keep.tile([P, 1], F32)
        nc.vector.tensor_scalar_max(out=divisor[:], in0=num[:], scalar1=1.0)
        one_over_num = keep.tile([P, 1], F32)
        nc.vector.reciprocal(out=one_over_num[:], in_=divisor[:])

        def mean_of_neigh(c):
            cols = slice(c * CHUNK, (c + 1) * CHUNK)
            slot_sum = work.tile([P, CHUNK], F32, tag="slot_sum")
            nc.vector.tensor_tensor(
                out=slot_sum[:], in0=neigh_slot[0][:, cols], in1=neigh_slot[1][:, cols], op=ALU.add
            )
            m_chunk = work.tile([P, CHUNK], BF16, tag="hidden_chunk")
            nc.scalar.activation(
                out=m_chunk[:], in_=slot_sum[:], func=ACT.Copy, scale=one_over_num[:, 0:1]
            )
            return m_chunk

        acc = [
            acc_pool.tile([P, width], F32, name="acc%d" % n) for n, width in enumerate(OUT_WIDTHS)
        ]

        def mx_pass(g, n, w_words):
            s, i = divmod(g, PLANES_PER_TILE)
            nc.tensor.matmul_mx(
                out=acc[n][:],
                lhsT=codes[:, g * P : (g + 1) * P].bitcast(FP8X4),
                lhsT_scale=code_scales[:, g * P : (g + 1) * P],
                rhs=w_words.bitcast(FP8X4),
                rhs_scale=w_planes[i * LIVE_ROWS : P, s, OUT_COLS[n]],
                start=(g == 0),
                stop=(g == PASSES - 1),
            )

        def whole_passes(first_pass, count):
            w_words = w_pool.tile([P, W_LOAD_PASSES, H], U32, align_bytes=64)
            nc.sync.dma_start(
                out=w_words[:, 0:count, :].bitcast(I32),
                in_=W_map_words[first_pass : first_pass + count]
                .rearrange("g p h t -> p g (h t)")
                .bitcast(I32),
            )
            for i in range(count):
                for n, cols in enumerate(OUT_COLS):
                    mx_pass(first_pass + i, n, w_words[:, i, cols])

        m_chunks = [mean_of_neigh(0)]
        for c in range(CHUNKS):
            whole_passes(c * W_LOAD_PASSES, W_LOAD_PASSES)
            if c + 1 < CHUNKS:
                m_chunks.append(mean_of_neigh(c + 1))
            quantise_chunk(m_chunks[c], SRC_PASSES + c * CHUNK_PASSES)
        first_tail = PASSES - TAPER_PASSES
        first_shrinking = first_tail - sum(SHRINKING_LOADS)
        for g in range(SRC_PASSES, first_shrinking, W_LOAD_PASSES):
            whole_passes(g, W_LOAD_PASSES)
        for i, count in enumerate(SHRINKING_LOADS):
            whole_passes(first_shrinking + sum(SHRINKING_LOADS[:i]), count)

        tail_words = []
        for n in range(N_BLOCKS):
            w_tail = tail_pool.tile([P, TAPER_PASSES, N_TILE], U32, align_bytes=64)
            nc.sync.dma_start(
                out=w_tail[:].bitcast(I32),
                in_=W_map_words[first_tail:PASSES, :, n * N_TILE : (n + 1) * N_TILE, :]
                .rearrange("g p h t -> p g (h t)")
                .bitcast(I32),
            )
            tail_words.append(w_tail)
        for block, parts in enumerate(BLOCK_PARTS):
            biased = work.tile([P, N_TILE], F32)
            result = work.tile([P, N_TILE], F32)

            def in_block(n):
                first = OUT_COLS[n].start - block * N_TILE
                return slice(first, first + OUT_WIDTHS[n])

            for n in parts:
                for i in range(TAPER_PASSES):
                    mx_pass(first_tail + i, n, tail_words[block][:, i, in_block(n)])
            for n in parts:
                nc.vector.tensor_tensor(
                    out=biased[:, in_block(n)],
                    in0=acc[n][:],
                    in1=bias_all[:, OUT_COLS[n]],
                    op=ALU.add,
                )
            for n in parts:
                nc.vector.scalar_tensor_tensor(
                    out=result[:, in_block(n)],
                    in0=biased[:, in_block(n)],
                    scalar=SLOPE,
                    in1=biased[:, in_block(n)],
                    op0=ALU.mult,
                    op1=ALU.max,
                )
                nc.sync.dma_start(out=out[:, OUT_COLS[n]], in_=result[:, in_block(n)])
